import numpy as np
import ml_dtypes


def mxq(x, axis, fmt="e4m3"):
    dtype, down = {"e4m3": (ml_dtypes.float8_e4m3fn, 7), "e5m2": (ml_dtypes.float8_e5m2, 14)}[fmt]
    v = np.moveaxis(np.asarray(x, np.float32).astype(ml_dtypes.bfloat16).astype(np.float64), axis, -1)
    blocks = v.reshape(v.shape[:-1] + (-1, 32))
    amax = np.abs(blocks).max(-1, keepdims=True)
    byte = np.maximum(np.where(amax > 0, np.frexp(amax)[1] - 1 + 127, 0) - down, 1)
    scale = np.exp2(byte - 127.0)
    codes = (blocks / scale).astype(np.float32).astype(dtype).astype(np.float64)
    return np.moveaxis((codes * scale).reshape(v.shape), -1, axis)


WIDE = False


def mx_kscale(k):
    if not WIDE:
        return np.ones(k)
    levels = np.array([30, -30])
    if k % 512:
        return np.exp2(np.random.permutation(np.resize(levels, k // 32))).repeat(32)
    a = np.empty((k // 512, 16))
    for p in range(k // 512):
        a[p, :8] = np.random.permutation(np.resize(levels, 8))
        for g in range(8):
            far = levels[np.abs(levels - a[p, g]) >= 10]
            a[p, g + 8] = far[np.random.randint(len(far))]
    return np.exp2(a.ravel()).repeat(32)


BF16 = ml_dtypes.bfloat16


def bf(x):
    return np.asarray(x, np.float32).astype(BF16)


def f64(x):
    return np.asarray(x).astype(np.float64)


B, T, C, N, D = 4, 128, 2048, 16, 128
ROPE_THETA = 10000.0


def rope_cos_sin():
    inv_freq = 1.0 / (ROPE_THETA ** (f64(np.arange(0, D, 2)) / D))
    freqs = np.outer(f64(np.arange(T)), inv_freq)
    return np.cos(freqs), np.sin(freqs)


def apply_rope(v, cos, sin):
    v1 = v[..., 0::2]
    v2 = v[..., 1::2]
    c = cos[None, :, None, :]
    s = sin[None, :, None, :]
    r1 = v1 * c - v2 * s
    r2 = v1 * s + v2 * c
    return np.stack([r1, r2], axis=-1).reshape(v.shape)


def setup_inputs():
    s = mx_kscale(C)
    return {"normalized_resid_pre": bf(np.random.standard_normal((B, T, C)) * s),
            "W_Q": bf(np.random.standard_normal((N, C, D)) / np.sqrt(C) / s[None, :, None]),
            "b_Q": bf(np.random.standard_normal((N, D)) * 0.2),
            "W_K": bf(np.random.standard_normal((N, C, D)) / np.sqrt(C) / s[None, :, None]),
            "b_K": bf(np.random.standard_normal((N, D)) * 0.2)}


def reference(normalized_resid_pre, W_Q, b_Q, W_K, b_K):
    xq = mxq(f64(normalized_resid_pre), 2, "e5m2").reshape(B * T, C)
    wq = mxq(f64(W_Q), 1, "e5m2").transpose(1, 0, 2).reshape(C, N * D)
    wk = mxq(f64(W_K), 1, "e5m2").transpose(1, 0, 2).reshape(C, N * D)
    Q = (xq @ wq).reshape(B, T, N, D) + f64(b_Q)
    K = (xq @ wk).reshape(B, T, N, D) + f64(b_K)
    cos, sin = rope_cos_sin()
    return apply_rope(Q, cos, sin), apply_rope(K, cos, sin)

@@ -1,0 +1,214 @@
+import math
+from contextlib import ExitStack
+
+import concourse.mybir as mybir
+from concourse.masks import make_identity
+
+B, T, C, N, D = 4, 128, 2048, 16, 128
+ROPE_THETA = 10000.0
+FLOPS = 2 * B * T * C * 2 * N * D
+
+F32 = mybir.dt.float32
+BF16 = mybir.dt.bfloat16
+I32 = mybir.dt.int32
+U32 = mybir.dt.uint32
+U8 = mybir.dt.uint8
+E5M2X4 = mybir.dt.float8_e5m2_x4
+ALU = mybir.AluOpType
+ACT = mybir.ActivationFunctionType
+
+P = 128
+PACK = 4
+K_PASS = P * PACK
+PASSES = C // K_PASS
+TOKENS = B * T
+HEADS = 2 * N
+PAIRS = HEADS // 2
+RUN = 4
+RUNS = D // RUN
+VECTOR_RUNS = 11
+VECTOR_RUNS_EARLY = 20
+EARLY_HEADS = 6
+LOAD_AHEAD = 6
+
+
+def tile_ropeattention_pa_kernel(tc, x, W_Q, b_Q, W_K, b_K, out_0, out_1):
+    nc = tc.nc
+
+    with ExitStack() as ctx:
+        keep = ctx.enter_context(tc.tile_pool(name="keep", bufs=1))
+        flow = ctx.enter_context(tc.tile_pool(name="flow", bufs=1))
+        psum = ctx.enter_context(tc.psum_pool(name="psum", bufs=4))
+        ctx.enter_context(tc.manual_schedule())
+
+        ident = keep.tile([P, P], F32)
+        swap = keep.tile([P, P], F32)
+        ident_bf = keep.tile([P, P], BF16)
+        trig = keep.tile([P, 2, B, T], F32)
+        bias_rows = keep.tile([P, D], BF16)
+        bias_cols = keep.tile([P, HEADS], F32)
+        x_raw = [keep.tile([T, B, K_PASS], BF16, name="x_raw%d" % g) for g in range(PASSES)]
+        x_grouped = [keep.tile([P, TOKENS * PACK], BF16, name="x_grouped%d" % g, align_bytes=64) for g in range(PASSES)]
+        x_codes = [keep.tile([P, TOKENS], U32, name="x_codes%d" % g, align_bytes=64) for g in range(PASSES)]
+        x_scales = [keep.tile([P, TOKENS], U8, name="x_scales%d" % g, align_bytes=64) for g in range(PASSES)]
+
+        w_raw, w_grouped, w_codes, w_scales, acc, terms, rotated, staged, x_turned = {}, {}, {}, {}, {}, {}, {}, {}, {}
+
+        def load_x(g):
+            nc.sync.dma_start(out=x_raw[g][:], in_=x[:, :, g * K_PASS : (g + 1) * K_PASS].rearrange("b t k -> t b k"))
+
+        def load_w(h):
+            w_raw[h] = flow.tile([P, PASSES, PACK * D], BF16, name="w_raw", bufs=8)
+            w_head = W_Q[h] if h < N else W_K[h - N]
+            nc.sync.dma_start(out=w_raw[h][:], in_=w_head.rearrange("(g p j) d -> p g (j d)", p=P, j=PACK))
+
+        def load_bias():
+            nc.sync.dma_start(out=bias_rows[0:N, :], in_=b_Q)
+            nc.sync.dma_start(out=bias_rows[N : 2 * N, :], in_=b_K)
+
+        def build_trig():
+            channel = keep.tile([P, 1], I32)
+            nc.gpsimd.iota(channel[:], [[0, 1]], base=0, channel_multiplier=1)
+            base = keep.tile([P, 1], F32)
+            nc.gpsimd.memset(base[:], ROPE_THETA)
+            position = keep.tile([P, T], F32)
+            nc.gpsimd.iota(position[:], [[1, T]], base=0, channel_multiplier=0, allow_small_or_imprecise_dtypes=True)
+            pair = keep.tile([P, 1], I32)
+            nc.vector.tensor_scalar(out=pair[:], in0=channel[:], scalar1=1, scalar2=None, op0=ALU.arith_shift_right)
+            odd = keep.tile([P, 1], I32)
+            nc.vector.tensor_scalar(out=odd[:], in0=channel[:], scalar1=1, scalar2=None, op0=ALU.bitwise_and)
+            exponent = keep.tile([P, 1], F32)
+            nc.vector.tensor_scalar(out=exponent[:], in0=pair[:], scalar1=-2.0 / D, scalar2=None, op0=ALU.mult)
+            sin_scale = keep.tile([P, 1], F32)
+            nc.vector.tensor_scalar(out=sin_scale[:], in0=odd[:], scalar1=4.0 * math.pi, scalar2=-2.0 * math.pi, op0=ALU.mult, op1=ALU.add)
+            theta = keep.tile([P, 1], F32)
+            nc.gpsimd.tensor_tensor(out=theta[:], in0=base[:], in1=exponent[:], op=ALU.pow)
+            turns = keep.tile([P, 2, T], F32)
+            nc.vector.tensor_scalar(out=turns[:, 1, :], in0=position[:], scalar1=theta[:], scalar2=0.5 / math.pi, op0=ALU.mult, op1=ALU.mult)
+            nc.vector.tensor_scalar(out=turns[:, 0, :], in0=turns[:, 1, :], scalar1=0.25, scalar2=None, op0=ALU.add)
+            whole = keep.tile([P, 2, T], I32)
+            nc.vector.tensor_copy(out=whole[:], in_=turns[:])
+            frac = keep.tile([P, 2, T], F32)
+            nc.vector.tensor_tensor(out=frac[:], in0=turns[:], in1=whole[:], op=ALU.subtract)
+            folded = keep.tile([P, 2, T], F32)
+            nc.vector.scalar_tensor_tensor(out=folded[:], in0=frac[:], scalar=0.5, in1=frac[:], op0=ALU.is_gt, op1=ALU.subtract)
+            nc.scalar.activation(out=trig[:, 0], in_=folded[:, 0:1, :].to_broadcast([P, B, T]), func=ACT.Sin, scale=-2.0 * math.pi)
+            nc.scalar.activation(out=trig[:, 1], in_=folded[:, 1:2, :].to_broadcast([P, B, T]), func=ACT.Sin, scale=sin_scale[:])
+
+        def build_matrices():
+            make_identity(nc, ident[:])
+            nc.gpsimd.memset(bias_rows[:], 0.0)
+            make_identity(nc, ident_bf[:])
+            nc.gpsimd.memset(swap[:], 0.0)
+            nc.gpsimd.affine_select(out=swap[:], in_=swap[:], compare_op=ALU.not_equal, fill=1.0, base=-1,
+                                    pattern=[[-2, P // 2], [1, 2]], channel_multiplier=1)
+
+        def turn_bias():
+            bank = psum.tile([P, P], BF16, name="bias_bank", tag="acc")
+            nc.tensor.transpose(bank[:], bias_rows[:], ident_bf[:])
+            nc.scalar.copy(out=bias_cols[:], in_=bank[:, 0:HEADS])
+
+        def turn_x(g):
+            words = x_raw[g][:].rearrange("t b k -> t (b k)").bitcast(F32)
+            half_words = K_PASS // 2
+            for half in range(2):
+                bank = psum.tile([P, 2, 2, T], F32, name="x_bank", tag="rot")
+                x_turned[g, half] = bank
+                for bb in range(2):
+                    first = (2 * half + bb) * half_words
+                    for u in range(2):
+                        nc.tensor.transpose(bank[:, bb, u, :], words[:, first + u : first + half_words : 2], ident[:])
+
+        def copy_x(g):
+            for half in range(2):
+                dst = x_grouped[g][:].bitcast(F32).rearrange("p (b t u) -> p b t u", b=B, u=2)
+                nc.scalar.copy(out=dst[:, 2 * half : 2 * half + 2], in_=x_turned[g, half][:].rearrange("p b u t -> p b t u"))
+
+        def quantize_x(g):
+            nc.vector.quantize_mx(out=x_codes[g][:].bitcast(E5M2X4), scales=x_scales[g][:], in_=x_grouped[g][:])
+
+        def interleave(h):
+            w_grouped[h] = flow.tile([P, PASSES * D * PACK], BF16, name="w_grouped", bufs=6, align_bytes=64)
+            split = VECTOR_RUNS_EARLY if h < EARLY_HEADS else VECTOR_RUNS
+            src = w_raw[h][:].rearrange("p g (j c i) -> p g c j i", j=PACK, i=RUN)
+            dst = w_grouped[h][:].rearrange("p (g c i j) -> p g c j i", g=PASSES, i=RUN, j=PACK)
+            nc.vector.tensor_copy(out=dst[:, :, 0:split], in_=src[:, :, 0:split])
+            nc.scalar.copy(out=dst[:, :, split:RUNS], in_=src[:, :, split:RUNS])
+
+        def quantize_w(h):
+            w_codes[h] = flow.tile([P, PASSES * D], U32, name="w_codes", bufs=4, align_bytes=64)
+            w_scales[h] = flow.tile([P, PASSES * D], U8, name="w_scales", bufs=4, align_bytes=64)
+            nc.vector.quantize_mx(out=w_codes[h][:].bitcast(E5M2X4), scales=w_scales[h][:], in_=w_grouped[h][:])
+
+        def project(h):
+            acc[h] = psum.tile([D, TOKENS], F32, name="acc", tag="acc")
+            for g in range(PASSES):
+                cols = slice(g * D, (g + 1) * D)
+                nc.tensor.matmul_mx(out=acc[h][:], lhsT=w_codes[h][:, cols].bitcast(E5M2X4), lhsT_scale=w_scales[h][:, cols],
+                                    rhs=x_codes[g][:].bitcast(E5M2X4), rhs_scale=x_scales[g][:],
+                                    start=(g == 0), stop=(g == PASSES - 1))
+
+        def scale_terms(h):
+            terms[h] = flow.tile([D, 2, TOKENS], F32, name="terms", bufs=4)
+            nc.vector.scalar_tensor_tensor(out=terms[h][:], in0=acc[h][:].unsqueeze(1).to_broadcast([D, 2, TOKENS]),
+                                           scalar=bias_cols[:, h : h + 1], in1=trig[:].rearrange("p s b t -> p s (b t)"),
+                                           op0=ALU.add, op1=ALU.mult)
+
+        def rotate(h):
+            rotated[h] = psum.tile([T, B, D], F32, name="rotated", tag="rot")
+            for b in range(B):
+                cols = slice(b * T, (b + 1) * T)
+                nc.tensor.matmul(rotated[h][:, b, :], lhsT=terms[h][:, 0, cols], rhs=ident[:], start=True, stop=False, is_transpose=True)
+                nc.tensor.matmul(rotated[h][:, b, :], lhsT=terms[h][:, 1, cols], rhs=swap[:], start=False, stop=True, is_transpose=True)
+
+        def stage(h):
+            if h % 2 == 0:
+                staged[h // 2] = flow.tile([T, B, 2, D], F32, name="staged", bufs=4)
+            nc.scalar.copy(out=staged[h // 2][:, :, h % 2, :], in_=rotated[h][:])
+
+        def store(i):
+            dest = out_0 if 2 * i < N else out_1
+            n0 = (2 * i) % N
+            nc.sync.dma_start(out=dest[:, :, n0 : n0 + 2, :].rearrange("b t n d -> t b n d"), in_=staged[i][:])
+
+        load_w(0)
+        for g in range(PASSES):
+            load_x(g)
+        build_trig()
+        build_matrices()
+        load_w(1)
+        load_bias()
+        for h in range(2, LOAD_AHEAD):
+            load_w(h)
+
+        interleave(0)
+        for g in range(PASSES):
+            turn_x(g)
+            copy_x(g)
+            if g == 0:
+                quantize_w(0)
+            quantize_x(g)
+        interleave(1)
+        turn_bias()
+
+        for i in range(-1, PAIRS + 1):
+            for h in (2 * i + 2 + LOAD_AHEAD, 2 * i + 3 + LOAD_AHEAD):
+                if h < HEADS:
+                    load_w(h)
+            for h in (2 * i + 4, 2 * i + 5):
+                if h < HEADS:
+                    interleave(h)
+                if 0 < h - 2 < HEADS:
+                    quantize_w(h - 2)
+            for h in (2 * i + 2, 2 * i + 3):
+                if h < HEADS:
+                    project(h)
+            if i >= 1:
+                stage(2 * i - 2)
+                stage(2 * i - 1)
+                store(i - 1)
+            if 0 <= i < PAIRS:
+                for h in (2 * i, 2 * i + 1):
+                    scale_terms(h)
+                for h in (2 * i, 2 * i + 1):
+                    rotate(h)

@@ -26,10 +26,11 @@ HEADS = 2 * N
 PAIRS = HEADS // 2
 RUN = 4
 RUNS = D // RUN
-VECTOR_RUNS = 11
-VECTOR_RUNS_EARLY = 20
-EARLY_HEADS = 6
-LOAD_AHEAD = 6
+VECTOR_RUNS = 10
+VECTOR_RUNS_EARLY = 16
+EARLY_HEADS = 3
+LOAD_AHEAD = 8
+STORE_GROUPS = [4] * 7 + [2, 1]
 
 
 def tile_ropeattention_pa_kernel(tc, x, W_Q, b_Q, W_K, b_K, out_0, out_1):
@@ -44,6 +45,7 @@ def tile_ropeattention_pa_kernel(tc, x, W_Q, b_Q, W_K, b_K, out_0, out_1):
         ident = keep.tile([P, P], F32)
         swap = keep.tile([P, P], F32)
         ident_bf = keep.tile([P, P], BF16)
+        trig_once = keep.tile([P, 2, T], F32)
         trig = keep.tile([P, 2, B, T], F32)
         bias_rows = keep.tile([P, D], BF16)
         bias_cols = keep.tile([P, HEADS], F32)
@@ -92,8 +94,11 @@ def tile_ropeattention_pa_kernel(tc, x, W_Q, b_Q, W_K, b_K, out_0, out_1):
             nc.vector.tensor_tensor(out=frac[:], in0=turns[:], in1=whole[:], op=ALU.subtract)
             folded = keep.tile([P, 2, T], F32)
             nc.vector.scalar_tensor_tensor(out=folded[:], in0=frac[:], scalar=0.5, in1=frac[:], op0=ALU.is_gt, op1=ALU.subtract)
-            nc.scalar.activation(out=trig[:, 0], in_=folded[:, 0:1, :].to_broadcast([P, B, T]), func=ACT.Sin, scale=-2.0 * math.pi)
-            nc.scalar.activation(out=trig[:, 1], in_=folded[:, 1:2, :].to_broadcast([P, B, T]), func=ACT.Sin, scale=sin_scale[:])
+            nc.scalar.activation(out=trig_once[:, 0, :], in_=folded[:, 0, :], func=ACT.Sin, scale=-2.0 * math.pi)
+            nc.scalar.activation(out=trig_once[:, 1, :], in_=folded[:, 1, :], func=ACT.Sin, scale=sin_scale[:])
+
+        def repeat_trig():
+            nc.vector.tensor_copy(out=trig[:], in_=trig_once[:].unsqueeze(2).to_broadcast([P, 2, B, T]))
 
         def build_matrices():
             make_identity(nc, ident[:])
@@ -128,12 +133,13 @@ def tile_ropeattention_pa_kernel(tc, x, W_Q, b_Q, W_K, b_K, out_0, out_1):
             nc.vector.quantize_mx(out=x_codes[g][:].bitcast(E5M2X4), scales=x_scales[g][:], in_=x_grouped[g][:])
 
         def interleave(h):
-            w_grouped[h] = flow.tile([P, PASSES * D * PACK], BF16, name="w_grouped", bufs=6, align_bytes=64)
-            split = VECTOR_RUNS_EARLY if h < EARLY_HEADS else VECTOR_RUNS
+            w_grouped[h] = flow.tile([P, PASSES * D * PACK], BF16, name="w_grouped", bufs=4, align_bytes=64)
+            split = RUNS if h == 0 else VECTOR_RUNS_EARLY if h < EARLY_HEADS else VECTOR_RUNS
             src = w_raw[h][:].rearrange("p g (j c i) -> p g c j i", j=PACK, i=RUN)
             dst = w_grouped[h][:].rearrange("p (g c i j) -> p g c j i", g=PASSES, i=RUN, j=PACK)
             nc.vector.tensor_copy(out=dst[:, :, 0:split], in_=src[:, :, 0:split])
-            nc.scalar.copy(out=dst[:, :, split:RUNS], in_=src[:, :, split:RUNS])
+            if split < RUNS:
+                nc.scalar.copy(out=dst[:, :, split:RUNS], in_=src[:, :, split:RUNS])
 
         def quantize_w(h):
             w_codes[h] = flow.tile([P, PASSES * D], U32, name="w_codes", bufs=4, align_bytes=64)
@@ -148,67 +154,82 @@ def tile_ropeattention_pa_kernel(tc, x, W_Q, b_Q, W_K, b_K, out_0, out_1):
                                     rhs=x_codes[g][:].bitcast(E5M2X4), rhs_scale=x_scales[g][:],
                                     start=(g == 0), stop=(g == PASSES - 1))
 
-        def scale_terms(h):
-            terms[h] = flow.tile([D, 2, TOKENS], F32, name="terms", bufs=4)
-            nc.vector.scalar_tensor_tensor(out=terms[h][:], in0=acc[h][:].unsqueeze(1).to_broadcast([D, 2, TOKENS]),
-                                           scalar=bias_cols[:, h : h + 1], in1=trig[:].rearrange("p s b t -> p s (b t)"),
+        def scale_terms(h, b0, b1):
+            cols = slice(b0 * T, b1 * T)
+            width = (b1 - b0) * T
+            terms[h, b0] = flow.tile([D, 2, width], F32, name="terms", bufs=4)
+            nc.vector.scalar_tensor_tensor(out=terms[h, b0][:], in0=acc[h][:, cols].unsqueeze(1).to_broadcast([D, 2, width]),
+                                           scalar=bias_cols[:, h : h + 1], in1=trig[:].rearrange("p s b t -> p s (b t)")[:, :, cols],
                                            op0=ALU.add, op1=ALU.mult)
 
-        def rotate(h):
-            rotated[h] = psum.tile([T, B, D], F32, name="rotated", tag="rot")
-            for b in range(B):
+        def rotate(h, b0, b1):
+            rotated[h, b0] = psum.tile([T, b1 - b0, D], F32, name="rotated", tag="rot")
+            for b in range(b1 - b0):
                 cols = slice(b * T, (b + 1) * T)
-                nc.tensor.matmul(rotated[h][:, b, :], lhsT=terms[h][:, 0, cols], rhs=ident[:], start=True, stop=False, is_transpose=True)
-                nc.tensor.matmul(rotated[h][:, b, :], lhsT=terms[h][:, 1, cols], rhs=swap[:], start=False, stop=True, is_transpose=True)
+                nc.tensor.matmul(rotated[h, b0][:, b, :], lhsT=terms[h, b0][:, 0, cols], rhs=ident[:], start=True, stop=False, is_transpose=True)
+                nc.tensor.matmul(rotated[h, b0][:, b, :], lhsT=terms[h, b0][:, 1, cols], rhs=swap[:], start=False, stop=True, is_transpose=True)
 
-        def stage(h):
-            if h % 2 == 0:
-                staged[h // 2] = flow.tile([T, B, 2, D], F32, name="staged", bufs=4)
-            nc.scalar.copy(out=staged[h // 2][:, :, h % 2, :], in_=rotated[h][:])
+        group_of = {}
+        first = 0
+        for size in STORE_GROUPS:
+            for h in range(first, first + size):
+                group_of[h] = (first, size)
+            first += size
 
-        def store(i):
-            dest = out_0 if 2 * i < N else out_1
-            n0 = (2 * i) % N
-            nc.sync.dma_start(out=dest[:, :, n0 : n0 + 2, :].rearrange("b t n d -> t b n d"), in_=staged[i][:])
+        def stage_and_store(h):
+            first, size = group_of[h]
+            if h == first:
+                staged[first] = flow.tile([T, B, size, D], F32, name="staged", bufs=3)
+            nc.scalar.copy(out=staged[first][:, :, h - first, :], in_=rotated[h, 0][:])
+            if h == first + size - 1:
+                dest = out_0 if first < N else out_1
+                n0 = first % N
+                nc.sync.dma_start(out=dest[:, :, n0 : n0 + size, :].rearrange("b t n d -> t b n d"), in_=staged[first][:])
+
+        def finish_last(b0, b1):
+            part = flow.tile([T, b1 - b0, D], F32, name="last_part", bufs=2)
+            nc.scalar.copy(out=part[:], in_=rotated[HEADS - 1, b0][:])
+            nc.sync.dma_start(out=out_1[b0:b1, :, N - 1, :].rearrange("b t d -> t b d"), in_=part[:])
 
         load_w(0)
         for g in range(PASSES):
             load_x(g)
         build_trig()
         build_matrices()
-        load_w(1)
         load_bias()
-        for h in range(2, LOAD_AHEAD):
+        for h in range(1, LOAD_AHEAD):
             load_w(h)
 
         interleave(0)
+        repeat_trig()
         for g in range(PASSES):
             turn_x(g)
             copy_x(g)
             if g == 0:
                 quantize_w(0)
+            if g == PASSES - 1:
+                interleave(1)
             quantize_x(g)
-        interleave(1)
         turn_bias()
+        project(0)
 
-        for i in range(-1, PAIRS + 1):
-            for h in (2 * i + 2 + LOAD_AHEAD, 2 * i + 3 + LOAD_AHEAD):
-                if h < HEADS:
-                    load_w(h)
-            for h in (2 * i + 4, 2 * i + 5):
-                if h < HEADS:
-                    interleave(h)
-                if 0 < h - 2 < HEADS:
-                    quantize_w(h - 2)
-            for h in (2 * i + 2, 2 * i + 3):
-                if h < HEADS:
-                    project(h)
-            if i >= 1:
-                stage(2 * i - 2)
-                stage(2 * i - 1)
-                store(i - 1)
-            if 0 <= i < PAIRS:
-                for h in (2 * i, 2 * i + 1):
-                    scale_terms(h)
-                for h in (2 * i, 2 * i + 1):
-                    rotate(h)
+        last = HEADS - 1
+        for j in range(-1, HEADS + 1):
+            if LOAD_AHEAD <= j + LOAD_AHEAD < HEADS:
+                load_w(j + LOAD_AHEAD)
+            if j + 3 < HEADS:
+                interleave(j + 3)
+            if j + 2 < HEADS:
+                quantize_w(j + 2)
+                project(j + 2)
+            if j >= 2:
+                stage_and_store(j - 2)
+            if 0 <= j < last:
+                scale_terms(j, 0, B)
+                rotate(j, 0, B)
+            if j == last:
+                for b0 in (0, B // 2):
+                    scale_terms(j, b0, b0 + B // 2)
+                    rotate(j, b0, b0 + B // 2)
+        for b0 in (0, B // 2):
+            finish_last(b0, b0 + B // 2)

@@ -26,10 +26,10 @@ HEADS = 2 * N
 PAIRS = HEADS // 2
 RUN = 4
 RUNS = D // RUN
-VECTOR_RUNS = 10
+VECTOR_RUNS = 11
 VECTOR_RUNS_EARLY = 16
-EARLY_HEADS = 3
-LOAD_AHEAD = 8
+UNITS = [(0, 1), (1, 1)] + [(h, 2) for h in range(2, HEADS - 2, 2)] + [(HEADS - 2, 1), (HEADS - 1, 1)]
+LOAD_AHEAD = 5
 STORE_GROUPS = [4] * 7 + [2, 1]
 
 
@@ -59,10 +59,11 @@ def tile_ropeattention_pa_kernel(tc, x, W_Q, b_Q, W_K, b_K, out_0, out_1):
         def load_x(g):
             nc.sync.dma_start(out=x_raw[g][:], in_=x[:, :, g * K_PASS : (g + 1) * K_PASS].rearrange("b t k -> t b k"))
 
-        def load_w(h):
-            w_raw[h] = flow.tile([P, PASSES, PACK * D], BF16, name="w_raw", bufs=8)
-            w_head = W_Q[h] if h < N else W_K[h - N]
-            nc.sync.dma_start(out=w_raw[h][:], in_=w_head.rearrange("(g p j) d -> p g (j d)", p=P, j=PACK))
+        def load_w(u):
+            h, count = UNITS[u]
+            w_raw[u] = flow.tile([P, count * PASSES, PACK * D], BF16, name="w_raw", bufs=4)
+            w_heads = W_Q[h : h + count] if h < N else W_K[h - N : h - N + count]
+            nc.sync.dma_start(out=w_raw[u][:], in_=w_heads.rearrange("n (g p j) d -> p (n g) (j d)", p=P, j=PACK))
 
         def load_bias():
             nc.sync.dma_start(out=bias_rows[0:N, :], in_=b_Q)
@@ -132,27 +133,32 @@ def tile_ropeattention_pa_kernel(tc, x, W_Q, b_Q, W_K, b_K, out_0, out_1):
         def quantize_x(g):
             nc.vector.quantize_mx(out=x_codes[g][:].bitcast(E5M2X4), scales=x_scales[g][:], in_=x_grouped[g][:])
 
-        def interleave(h):
-            w_grouped[h] = flow.tile([P, PASSES * D * PACK], BF16, name="w_grouped", bufs=4, align_bytes=64)
-            split = RUNS if h == 0 else VECTOR_RUNS_EARLY if h < EARLY_HEADS else VECTOR_RUNS
-            src = w_raw[h][:].rearrange("p g (j c i) -> p g c j i", j=PACK, i=RUN)
-            dst = w_grouped[h][:].rearrange("p (g c i j) -> p g c j i", g=PASSES, i=RUN, j=PACK)
+        def interleave(u):
+            count = UNITS[u][1]
+            w_grouped[u] = flow.tile([P, count * PASSES * D * PACK], BF16, name="w_grouped", bufs=3, align_bytes=64)
+            split = RUNS if u == 0 else VECTOR_RUNS_EARLY if u == 1 else VECTOR_RUNS
+            src = w_raw[u][:].rearrange("p g (j c i) -> p g c j i", j=PACK, i=RUN)
+            dst = w_grouped[u][:].rearrange("p (g c i j) -> p g c j i", c=RUNS, i=RUN, j=PACK)
             nc.vector.tensor_copy(out=dst[:, :, 0:split], in_=src[:, :, 0:split])
             if split < RUNS:
                 nc.scalar.copy(out=dst[:, :, split:RUNS], in_=src[:, :, split:RUNS])
 
-        def quantize_w(h):
-            w_codes[h] = flow.tile([P, PASSES * D], U32, name="w_codes", bufs=4, align_bytes=64)
-            w_scales[h] = flow.tile([P, PASSES * D], U8, name="w_scales", bufs=4, align_bytes=64)
-            nc.vector.quantize_mx(out=w_codes[h][:].bitcast(E5M2X4), scales=w_scales[h][:], in_=w_grouped[h][:])
+        def quantize_w(u):
+            count = UNITS[u][1]
+            w_codes[u] = flow.tile([P, count * PASSES * D], U32, name="w_codes", bufs=3, align_bytes=64)
+            w_scales[u] = flow.tile([P, count * PASSES * D], U8, name="w_scales", bufs=3, align_bytes=64)
+            nc.vector.quantize_mx(out=w_codes[u][:].bitcast(E5M2X4), scales=w_scales[u][:], in_=w_grouped[u][:])
 
-        def project(h):
-            acc[h] = psum.tile([D, TOKENS], F32, name="acc", tag="acc")
-            for g in range(PASSES):
-                cols = slice(g * D, (g + 1) * D)
-                nc.tensor.matmul_mx(out=acc[h][:], lhsT=w_codes[h][:, cols].bitcast(E5M2X4), lhsT_scale=w_scales[h][:, cols],
-                                    rhs=x_codes[g][:].bitcast(E5M2X4), rhs_scale=x_scales[g][:],
-                                    start=(g == 0), stop=(g == PASSES - 1))
+        def project(u):
+            h0, count = UNITS[u]
+            for h in range(h0, h0 + count):
+                acc[h] = psum.tile([D, TOKENS], F32, name="acc", tag="acc")
+                for g in range(PASSES):
+                    first_col = ((h - h0) * PASSES + g) * D
+                    cols = slice(first_col, first_col + D)
+                    nc.tensor.matmul_mx(out=acc[h][:], lhsT=w_codes[u][:, cols].bitcast(E5M2X4), lhsT_scale=w_scales[u][:, cols],
+                                        rhs=x_codes[g][:].bitcast(E5M2X4), rhs_scale=x_scales[g][:],
+                                        start=(g == 0), stop=(g == PASSES - 1))
 
         def scale_terms(h, b0, b1):
             cols = slice(b0 * T, b1 * T)
@@ -197,8 +203,8 @@ def tile_ropeattention_pa_kernel(tc, x, W_Q, b_Q, W_K, b_K, out_0, out_1):
         build_trig()
         build_matrices()
         load_bias()
-        for h in range(1, LOAD_AHEAD):
-            load_w(h)
+        for u in range(1, LOAD_AHEAD - 1):
+            load_w(u)
 
         interleave(0)
         repeat_trig()
@@ -213,23 +219,29 @@ def tile_ropeattention_pa_kernel(tc, x, W_Q, b_Q, W_K, b_K, out_0, out_1):
         turn_bias()
         project(0)
 
-        last = HEADS - 1
-        for j in range(-1, HEADS + 1):
-            if LOAD_AHEAD <= j + LOAD_AHEAD < HEADS:
-                load_w(j + LOAD_AHEAD)
-            if j + 3 < HEADS:
-                interleave(j + 3)
-            if j + 2 < HEADS:
-                quantize_w(j + 2)
-                project(j + 2)
-            if j >= 2:
-                stage_and_store(j - 2)
-            if 0 <= j < last:
-                scale_terms(j, 0, B)
-                rotate(j, 0, B)
-            if j == last:
+        last = len(UNITS) - 1
+        load_w(LOAD_AHEAD - 1)
+        for u in range(len(UNITS)):
+            if u + LOAD_AHEAD <= last:
+                load_w(u + LOAD_AHEAD)
+            if u + 2 <= last:
+                interleave(u + 2)
+            if u + 1 <= last:
+                quantize_w(u + 1)
+                project(u + 1)
+            if u >= 1:
+                h0, count = UNITS[u - 1]
+                for h in range(h0, h0 + count):
+                    stage_and_store(h)
+            h0, count = UNITS[u]
+            if u < last:
+                for h in range(h0, h0 + count):
+                    scale_terms(h, 0, B)
+                for h in range(h0, h0 + count):
+                    rotate(h, 0, B)
+            else:
                 for b0 in (0, B // 2):
-                    scale_terms(j, b0, b0 + B // 2)
-                    rotate(j, b0, b0 + B // 2)
+                    scale_terms(h0, b0, b0 + B // 2)
+                    rotate(h0, b0, b0 + B // 2)
         for b0 in (0, B // 2):
             finish_last(b0, b0 + B // 2)

import math
from contextlib import ExitStack

import concourse.mybir as mybir
from concourse.masks import make_identity

B, T, C, N, D = 4, 128, 2048, 16, 128
ROPE_THETA = 10000.0
FLOPS = 2 * B * T * C * 2 * N * D

F32 = mybir.dt.float32
BF16 = mybir.dt.bfloat16
I32 = mybir.dt.int32
U32 = mybir.dt.uint32
U8 = mybir.dt.uint8
E5M2X4 = mybir.dt.float8_e5m2_x4
ALU = mybir.AluOpType
ACT = mybir.ActivationFunctionType

P = 128
PACK = 4
K_PASS = P * PACK
PASSES = C // K_PASS
TOKENS = B * T
HEADS = 2 * N
PAIRS = HEADS // 2
RUN = 4
RUNS = D // RUN
VECTOR_RUNS = 11
VECTOR_RUNS_EARLY = 16
UNITS = [(0, 1), (1, 1)] + [(h, 2) for h in range(2, HEADS - 2, 2)] + [(HEADS - 2, 1), (HEADS - 1, 1)]
LOAD_AHEAD = 5
STORE_GROUPS = [4] * 7 + [2, 1]


def tile_ropeattention_pa_kernel(tc, x, W_Q, b_Q, W_K, b_K, out_0, out_1):
    nc = tc.nc

    with ExitStack() as ctx:
        keep = ctx.enter_context(tc.tile_pool(name="keep", bufs=1))
        flow = ctx.enter_context(tc.tile_pool(name="flow", bufs=1))
        psum = ctx.enter_context(tc.psum_pool(name="psum", bufs=4))
        ctx.enter_context(tc.manual_schedule())

        ident = keep.tile([P, P], F32)
        swap = keep.tile([P, P], F32)
        ident_bf = keep.tile([P, P], BF16)
        trig_once = keep.tile([P, 2, T], F32)
        trig = keep.tile([P, 2, B, T], F32)
        bias_rows = keep.tile([P, D], BF16)
        bias_cols = keep.tile([P, HEADS], F32)
        x_raw = [keep.tile([T, B, K_PASS], BF16, name="x_raw%d" % g) for g in range(PASSES)]
        x_grouped = [keep.tile([P, TOKENS * PACK], BF16, name="x_grouped%d" % g, align_bytes=64) for g in range(PASSES)]
        x_codes = [keep.tile([P, TOKENS], U32, name="x_codes%d" % g, align_bytes=64) for g in range(PASSES)]
        x_scales = [keep.tile([P, TOKENS], U8, name="x_scales%d" % g, align_bytes=64) for g in range(PASSES)]

        w_raw, w_grouped, w_codes, w_scales, acc, terms, rotated, staged, x_turned = {}, {}, {}, {}, {}, {}, {}, {}, {}

        def load_x(g):
            nc.sync.dma_start(out=x_raw[g][:], in_=x[:, :, g * K_PASS : (g + 1) * K_PASS].rearrange("b t k -> t b k"))

        def load_w(u):
            h, count = UNITS[u]
            w_raw[u] = flow.tile([P, count * PASSES, PACK * D], BF16, name="w_raw", bufs=4)
            w_heads = W_Q[h : h + count] if h < N else W_K[h - N : h - N + count]
            nc.sync.dma_start(out=w_raw[u][:], in_=w_heads.rearrange("n (g p j) d -> p (n g) (j d)", p=P, j=PACK))

        def load_bias():
            nc.sync.dma_start(out=bias_rows[0:N, :], in_=b_Q)
            nc.sync.dma_start(out=bias_rows[N : 2 * N, :], in_=b_K)

        def build_trig():
            channel = keep.tile([P, 1], I32)
            nc.gpsimd.iota(channel[:], [[0, 1]], base=0, channel_multiplier=1)
            base = keep.tile([P, 1], F32)
            nc.gpsimd.memset(base[:], ROPE_THETA)
            position = keep.tile([P, T], F32)
            nc.gpsimd.iota(position[:], [[1, T]], base=0, channel_multiplier=0, allow_small_or_imprecise_dtypes=True)
            pair = keep.tile([P, 1], I32)
            nc.vector.tensor_scalar(out=pair[:], in0=channel[:], scalar1=1, scalar2=None, op0=ALU.arith_shift_right)
            odd = keep.tile([P, 1], I32)
            nc.vector.tensor_scalar(out=odd[:], in0=channel[:], scalar1=1, scalar2=None, op0=ALU.bitwise_and)
            exponent = keep.tile([P, 1], F32)
            nc.vector.tensor_scalar(out=exponent[:], in0=pair[:], scalar1=-2.0 / D, scalar2=None, op0=ALU.mult)
            sin_scale = keep.tile([P, 1], F32)
            nc.vector.tensor_scalar(out=sin_scale[:], in0=odd[:], scalar1=4.0 * math.pi, scalar2=-2.0 * math.pi, op0=ALU.mult, op1=ALU.add)
            theta = keep.tile([P, 1], F32)
            nc.gpsimd.tensor_tensor(out=theta[:], in0=base[:], in1=exponent[:], op=ALU.pow)
            turns = keep.tile([P, 2, T], F32)
            nc.vector.tensor_scalar(out=turns[:, 1, :], in0=position[:], scalar1=theta[:], scalar2=0.5 / math.pi, op0=ALU.mult, op1=ALU.mult)
            nc.vector.tensor_scalar(out=turns[:, 0, :], in0=turns[:, 1, :], scalar1=0.25, scalar2=None, op0=ALU.add)
            whole = keep.tile([P, 2, T], I32)
            nc.vector.tensor_copy(out=whole[:], in_=turns[:])
            frac = keep.tile([P, 2, T], F32)
            nc.vector.tensor_tensor(out=frac[:], in0=turns[:], in1=whole[:], op=ALU.subtract)
            folded = keep.tile([P, 2, T], F32)
            nc.vector.scalar_tensor_tensor(out=folded[:], in0=frac[:], scalar=0.5, in1=frac[:], op0=ALU.is_gt, op1=ALU.subtract)
            nc.scalar.activation(out=trig_once[:, 0, :], in_=folded[:, 0, :], func=ACT.Sin, scale=-2.0 * math.pi)
            nc.scalar.activation(out=trig_once[:, 1, :], in_=folded[:, 1, :], func=ACT.Sin, scale=sin_scale[:])

        def repeat_trig():
            nc.vector.tensor_copy(out=trig[:], in_=trig_once[:].unsqueeze(2).to_broadcast([P, 2, B, T]))

        def build_matrices():
            make_identity(nc, ident[:])
            nc.gpsimd.memset(bias_rows[:], 0.0)
            make_identity(nc, ident_bf[:])
            nc.gpsimd.memset(swap[:], 0.0)
            nc.gpsimd.affine_select(out=swap[:], in_=swap[:], compare_op=ALU.not_equal, fill=1.0, base=-1,
                                    pattern=[[-2, P // 2], [1, 2]], channel_multiplier=1)

        def turn_bias():
            bank = psum.tile([P, P], BF16, name="bias_bank", tag="acc")
            nc.tensor.transpose(bank[:], bias_rows[:], ident_bf[:])
            nc.scalar.copy(out=bias_cols[:], in_=bank[:, 0:HEADS])

        def turn_x(g):
            words = x_raw[g][:].rearrange("t b k -> t (b k)").bitcast(F32)
            half_words = K_PASS // 2
            for half in range(2):
                bank = psum.tile([P, 2, 2, T], F32, name="x_bank", tag="rot")
                x_turned[g, half] = bank
                for bb in range(2):
                    first = (2 * half + bb) * half_words
                    for u in range(2):
                        nc.tensor.transpose(bank[:, bb, u, :], words[:, first + u : first + half_words : 2], ident[:])

        def copy_x(g):
            for half in range(2):
                dst = x_grouped[g][:].bitcast(F32).rearrange("p (b t u) -> p b t u", b=B, u=2)
                nc.scalar.copy(out=dst[:, 2 * half : 2 * half + 2], in_=x_turned[g, half][:].rearrange("p b u t -> p b t u"))

        def quantize_x(g):
            nc.vector.quantize_mx(out=x_codes[g][:].bitcast(E5M2X4), scales=x_scales[g][:], in_=x_grouped[g][:])

        def interleave(u):
            count = UNITS[u][1]
            w_grouped[u] = flow.tile([P, count * PASSES * D * PACK], BF16, name="w_grouped", bufs=3, align_bytes=64)
            split = RUNS if u == 0 else VECTOR_RUNS_EARLY if u == 1 else VECTOR_RUNS
            src = w_raw[u][:].rearrange("p g (j c i) -> p g c j i", j=PACK, i=RUN)
            dst = w_grouped[u][:].rearrange("p (g c i j) -> p g c j i", c=RUNS, i=RUN, j=PACK)
            nc.vector.tensor_copy(out=dst[:, :, 0:split], in_=src[:, :, 0:split])
            if split < RUNS:
                nc.scalar.copy(out=dst[:, :, split:RUNS], in_=src[:, :, split:RUNS])

        def quantize_w(u):
            count = UNITS[u][1]
            w_codes[u] = flow.tile([P, count * PASSES * D], U32, name="w_codes", bufs=3, align_bytes=64)
            w_scales[u] = flow.tile([P, count * PASSES * D], U8, name="w_scales", bufs=3, align_bytes=64)
            nc.vector.quantize_mx(out=w_codes[u][:].bitcast(E5M2X4), scales=w_scales[u][:], in_=w_grouped[u][:])

        def project(u):
            h0, count = UNITS[u]
            for h in range(h0, h0 + count):
                acc[h] = psum.tile([D, TOKENS], F32, name="acc", tag="acc")
                for g in range(PASSES):
                    first_col = ((h - h0) * PASSES + g) * D
                    cols = slice(first_col, first_col + D)
                    nc.tensor.matmul_mx(out=acc[h][:], lhsT=w_codes[u][:, cols].bitcast(E5M2X4), lhsT_scale=w_scales[u][:, cols],
                                        rhs=x_codes[g][:].bitcast(E5M2X4), rhs_scale=x_scales[g][:],
                                        start=(g == 0), stop=(g == PASSES - 1))

        def scale_terms(h, b0, b1):
            cols = slice(b0 * T, b1 * T)
            width = (b1 - b0) * T
            terms[h, b0] = flow.tile([D, 2, width], F32, name="terms", bufs=4)
            nc.vector.scalar_tensor_tensor(out=terms[h, b0][:], in0=acc[h][:, cols].unsqueeze(1).to_broadcast([D, 2, width]),
                                           scalar=bias_cols[:, h : h + 1], in1=trig[:].rearrange("p s b t -> p s (b t)")[:, :, cols],
                                           op0=ALU.add, op1=ALU.mult)

        def rotate(h, b0, b1):
            rotated[h, b0] = psum.tile([T, b1 - b0, D], F32, name="rotated", tag="rot")
            for b in range(b1 - b0):
                cols = slice(b * T, (b + 1) * T)
                nc.tensor.matmul(rotated[h, b0][:, b, :], lhsT=terms[h, b0][:, 0, cols], rhs=ident[:], start=True, stop=False, is_transpose=True)
                nc.tensor.matmul(rotated[h, b0][:, b, :], lhsT=terms[h, b0][:, 1, cols], rhs=swap[:], start=False, stop=True, is_transpose=True)

        group_of = {}
        first = 0
        for size in STORE_GROUPS:
            for h in range(first, first + size):
                group_of[h] = (first, size)
            first += size

        def stage_and_store(h):
            first, size = group_of[h]
            if h == first:
                staged[first] = flow.tile([T, B, size, D], F32, name="staged", bufs=3)
            nc.scalar.copy(out=staged[first][:, :, h - first, :], in_=rotated[h, 0][:])
            if h == first + size - 1:
                dest = out_0 if first < N else out_1
                n0 = first % N
                nc.sync.dma_start(out=dest[:, :, n0 : n0 + size, :].rearrange("b t n d -> t b n d"), in_=staged[first][:])

        def finish_last(b0, b1):
            part = flow.tile([T, b1 - b0, D], F32, name="last_part", bufs=2)
            nc.scalar.copy(out=part[:], in_=rotated[HEADS - 1, b0][:])
            nc.sync.dma_start(out=out_1[b0:b1, :, N - 1, :].rearrange("b t d -> t b d"), in_=part[:])

        load_w(0)
        for g in range(PASSES):
            load_x(g)
        build_trig()
        build_matrices()
        load_bias()
        for u in range(1, LOAD_AHEAD - 1):
            load_w(u)

        interleave(0)
        repeat_trig()
        for g in range(PASSES):
            turn_x(g)
            copy_x(g)
            if g == 0:
                quantize_w(0)
            if g == PASSES - 1:
                interleave(1)
            quantize_x(g)
        turn_bias()
        project(0)

        last = len(UNITS) - 1
        load_w(LOAD_AHEAD - 1)
        for u in range(len(UNITS)):
            if u + LOAD_AHEAD <= last:
                load_w(u + LOAD_AHEAD)
            if u + 2 <= last:
                interleave(u + 2)
            if u + 1 <= last:
                quantize_w(u + 1)
                project(u + 1)
            if u >= 1:
                h0, count = UNITS[u - 1]
                for h in range(h0, h0 + count):
                    stage_and_store(h)
            h0, count = UNITS[u]
            if u < last:
                for h in range(h0, h0 + count):
                    scale_terms(h, 0, B)
                for h in range(h0, h0 + count):
                    rotate(h, 0, B)
            else:
                for b0 in (0, B // 2):
                    scale_terms(h0, b0, b0 + B // 2)
                    rotate(h0, b0, b0 + B // 2)
        for b0 in (0, B // 2):
            finish_last(b0, b0 + B // 2)
